import numpy as np
import ml_dtypes


def mxq(x, axis, fmt="e4m3"):
    dtype, down = {"e4m3": (ml_dtypes.float8_e4m3fn, 7), "e5m2": (ml_dtypes.float8_e5m2, 14)}[fmt]
    v = np.moveaxis(np.asarray(x, np.float32).astype(ml_dtypes.bfloat16).astype(np.float64), axis, -1)
    blocks = v.reshape(v.shape[:-1] + (-1, 32))
    amax = np.abs(blocks).max(-1, keepdims=True)
    byte = np.maximum(np.where(amax > 0, np.frexp(amax)[1] - 1 + 127, 0) - down, 1)
    scale = np.exp2(byte - 127.0)
    codes = (blocks / scale).astype(np.float32).astype(dtype).astype(np.float64)
    return np.moveaxis((codes * scale).reshape(v.shape), -1, axis)


WIDE = False


def mx_kscale(k):
    if not WIDE:
        return np.ones(k)
    levels = np.array([10, -10, 5, -5, 0])
    if k % 512:
        return np.exp2(np.random.permutation(np.resize(levels, k // 32))).repeat(32)
    a = np.empty((k // 512, 16))
    for p in range(k // 512):
        a[p, :8] = np.random.permutation(np.resize(levels, 8))
        for g in range(8):
            far = levels[np.abs(levels - a[p, g]) >= 10]
            a[p, g + 8] = far[np.random.randint(len(far))]
    return np.exp2(a.ravel()).repeat(32)


BF16 = ml_dtypes.bfloat16


def bf(x):
    return np.asarray(x, np.float32).astype(BF16)


def f64(x):
    return np.asarray(x).astype(np.float64)


N = 1536


def setup_inputs():
    s = mx_kscale(N)
    return {"A": bf(np.random.standard_normal((N, N)) * s), "B": bf(np.random.standard_normal((N, N)) * 1.5 / np.sqrt(N) / s[:, None])}


def reference(A, B):
    C = mxq(np.triu(f64(A)), 1, "e4m3") @ mxq(np.triu(f64(B)), 0, "e4m3")
    return np.triu(C)

@@ -1,0 +1,246 @@
+from contextlib import ExitStack
+
+import concourse.mybir as mybir
+from concourse.masks import make_identity
+
+FP8X4 = mybir.dt.float8_e4m3fn_x4
+BF16 = mybir.dt.bfloat16
+F32 = mybir.dt.float32
+I32 = mybir.dt.int32
+U32 = mybir.dt.uint32
+U8 = mybir.dt.uint8
+ALU = mybir.AluOpType
+
+N = 1536
+P = 128
+KP = 512
+NG = N // KP
+
+FLOPS = 2 * N * (N + 1) * (N + 2) // 6
+BYTES = 2 * (N * (N + 1) // 2) * 2 + N * N * 4
+
+PIECES = {0: [(0, 512)], 1: [(128, 128), (256, 256)], 2: [(256, 256)], 3: [(384, 128)]}
+
+
+def o_lo(i):
+    return 0 if i < 8 else 2 * KP
+
+
+def slot(first, second):
+    base = {2: 0, 1: 1, 0: 3}
+    return base[first] + second - first
+
+
+def tile_modelnew_kernel(tc, A, B, out):
+    nc = tc.nc
+    with ExitStack() as ctx:
+        const = ctx.enter_context(tc.tile_pool(name="const", bufs=1))
+        keep = ctx.enter_context(tc.tile_pool(name="keep", bufs=1))
+        psum = ctx.enter_context(tc.psum_pool(name="psum", bufs=1))
+        ctx.enter_context(tc.manual_schedule())
+
+        a_sb = {}
+        o_sb = {}
+        o_low = keep.tile([P, 4, KP], F32, name="o_low")
+        for i in range(12):
+            a_sb[i] = keep.tile([P, N - KP * (i // 4)], BF16, name="a_sb%d" % i)
+            if i < 8:
+                o_sb[i] = keep.tile([P, N], F32, name="o_sb%d" % i)
+            else:
+                o_sb[i] = o_low[:, i - 8, :]
+        b_raw = {}
+        for c in range(NG):
+            b_raw[c] = keep.tile([P, 4, N - KP * c], BF16, name="b_raw%d" % c)
+        ga = {}
+        gb = {}
+        for s in range(6):
+            ga[s] = keep.tile([P, 4 * KP], BF16, name="ga%d" % s, align_bytes=64)
+            gb[s] = keep.tile([P, KP, 4], BF16, name="gb%d" % s, align_bytes=64)
+        a_cod = keep.tile([P, 6, KP], U32, name="a_cod", align_bytes=64)
+        a_scl = keep.tile([P, 6, KP], U8, name="a_scl", align_bytes=64)
+        b_cod = keep.tile([P, 6, KP], U32, name="b_cod", align_bytes=64)
+        b_scl = keep.tile([P, 6, KP], U8, name="b_scl", align_bytes=64)
+        zeros = const.tile([P, 2 * KP], F32, name="zeros")
+        ident = const.tile([P, P], F32, name="ident")
+        mf = const.tile([P, 1088], F32, name="mf")
+        mw = const.tile([P, 1088], I32, name="mw")
+        mask_a = mw[:, 0:64]
+        mask_b = mw[:, 64:1088].rearrange("p (t x) -> p t x", t=4)
+        banks = [0]
+
+        def bank(shape):
+            n = banks[0]
+            banks[0] = n + 1
+            return psum.tile(shape, F32, name="bk%d_%d" % (n % 8, n), tag="bk%d" % (n % 8))
+
+        def load_a(g):
+            for r in range(4):
+                i = 4 * g + r
+                nc.sync.dma_start(out=a_sb[i][:, P * r :], in_=A[P * i : P * i + P, P * i : N])
+
+        def load_b(g):
+            k0 = KP * g
+            nc.sync.dma_start(out=b_raw[g][:], in_=B[k0 : k0 + KP, k0:N].rearrange("(p t) w -> p t w", t=4))
+
+        def mask_a_blocks(g):
+            for r in range(4):
+                blk = a_sb[4 * g + r][:, P * r : P * r + P].bitcast(I32)
+                nc.vector.tensor_tensor(out=blk, in0=blk, in1=mask_a, op=ALU.bitwise_and)
+
+        def mask_b_blocks(g):
+            blk = b_raw[g][:, :, 0:KP].bitcast(I32)
+            nc.vector.tensor_tensor(out=blk, in0=blk, in1=mask_b, op=ALU.bitwise_and)
+
+        def transpose_a(g, c):
+            gaf = ga[slot(g, c)][:].bitcast(F32)
+            for b in range(2):
+                xt = bank([P, 2, 2, P])
+                for q in range(2):
+                    af = a_sb[4 * g + 2 * b + q][:].bitcast(F32)
+                    for u in range(2):
+                        w0 = 256 * (c - g)
+                        nc.tensor.transpose(xt[:, q, u, :], af[:, w0 + u : w0 + 256 : 2], ident[:])
+                nc.scalar.copy(
+                    out=gaf[:, 512 * b : 512 * b + 512].rearrange("p (q i u) -> p q i u", q=2, u=2),
+                    in_=xt[:].rearrange("p q u i -> p q i u"),
+                )
+
+        def quant_a(g, c):
+            s = slot(g, c)
+            nc.vector.quantize_mx(out=a_cod[:, s, :].bitcast(FP8X4), scales=a_scl[:, s, :], in_=ga[s][:])
+
+        def regroup_b(c, j):
+            src = b_raw[c][:, :, KP * (j - c) : KP * (j - c) + KP]
+            nc.vector.tensor_copy(
+                out=gb[slot(c, j)][:].rearrange("p (c i) t -> p c t i", i=4),
+                in_=src.rearrange("p t (c i) -> p c t i", i=4),
+            )
+
+        def quant_b(c, j):
+            s = slot(c, j)
+            nc.vector.quantize_mx(
+                out=b_cod[:, s, :].bitcast(FP8X4), scales=b_scl[:, s, :],
+                in_=gb[s][:].rearrange("p w t -> p (w t)"),
+            )
+
+        def mx(acc, g, r, c, j, off, wid, start, stop):
+            sa = slot(g, c)
+            sb = slot(c, j)
+            rows = slice(P * r, P * r + P)
+            nc.tensor.matmul_mx(
+                out=acc[:, off : off + wid],
+                lhsT=a_cod[:, sa, rows].bitcast(FP8X4), lhsT_scale=a_scl[:, sa, rows],
+                rhs=b_cod[:, sb, off : off + wid].bitcast(FP8X4), rhs_scale=b_scl[:, sb, off : off + wid],
+                start=start, stop=stop,
+            )
+
+        def evac(eng, acc, g, r, j, lo):
+            i = 4 * g + r
+            dst = o_sb[i][:, KP * j + lo - o_lo(i) : KP * j + KP - o_lo(i)]
+            if eng == "v":
+                nc.vector.tensor_copy(out=dst, in_=acc[:, lo:KP])
+            else:
+                nc.scalar.copy(out=dst, in_=acc[:, lo:KP])
+
+        def diag_tile(g, r, eng):
+            acc = bank([P, KP])
+            for off, wid in PIECES[r]:
+                mx(acc, g, r, g, g, off, wid, True, True)
+            evac(eng, acc, g, r, g, P * r)
+
+        def open_tiles():
+            return [bank([P, KP]) for r in range(4)]
+
+        def passes(accs, g, c, j, start, stop):
+            for r in range(4):
+                mx(accs[r], g, r, c, j, 0, KP, start, stop)
+
+        def zero_prefix(rows):
+            for i in rows:
+                nc.scalar.copy(out=o_sb[i][:, 0 : P * i - o_lo(i)], in_=zeros[:, 0 : P * i - o_lo(i)])
+
+        def store(i):
+            nc.sync.dma_start(out=out[P * i : P * i + P, o_lo(i) : N], in_=o_sb[i][:])
+
+        nc.vector.memset(zeros[:], 0.0)
+        for g in (2, 1, 0):
+            for r in range(1, 4):
+                nc.vector.memset(a_sb[4 * g + r][:, 0 : P * r].bitcast(I32), 0)
+        for g in (2, 1, 0):
+            load_a(g)
+            load_b(g)
+        nc.sync.dma_start(
+            out=out[2 * KP : N, 0 : 2 * KP].rearrange("(r p) w -> p r w", p=P),
+            in_=zeros[:].unsqueeze(1).to_broadcast([P, 4, 2 * KP]),
+        )
+        zero_prefix([9, 10, 11, 4, 5, 6, 7])
+        nc.gpsimd.memset(mf[:], -1.0)
+        for lo_hi, fill in ((0, -65536.0), (1, 0.0)):
+            nc.gpsimd.affine_select(
+                out=mf[:, 0:64], in_=mf[:, 0:64], pattern=[[2, 64]], compare_op=ALU.is_ge,
+                fill=fill, base=lo_hi, channel_multiplier=-1,
+            )
+            nc.gpsimd.affine_select(
+                out=mf[:, 64:1088], in_=mf[:, 64:1088], pattern=[[-1, 4], [2, 256]], compare_op=ALU.is_ge,
+                fill=fill, base=lo_hi, channel_multiplier=-4,
+            )
+        make_identity(nc, ident[:])
+        nc.vector.tensor_copy(out=mw[:], in_=mf[:])
+
+        mask_a_blocks(2)
+        transpose_a(2, 2)
+        mask_b_blocks(2)
+        regroup_b(2, 2)
+        mask_a_blocks(1)
+        transpose_a(1, 1)
+        transpose_a(1, 2)
+        quant_b(2, 2)
+        quant_a(2, 2)
+        for r in range(4):
+            diag_tile(2, r, "s")
+        nc.sync.dma_start(out=out[2 * KP : N, 2 * KP : N].rearrange("(r p) w -> p r w", p=P), in_=o_low[:])
+        zero_prefix([1, 2, 3])
+
+        mask_b_blocks(1)
+        regroup_b(1, 1)
+        quant_a(1, 1)
+        regroup_b(1, 2)
+        mask_a_blocks(0)
+        for c in (1, 2, 0):
+            transpose_a(0, c)
+        quant_b(1, 1)
+        for r in range(4):
+            diag_tile(1, r, "s")
+        quant_a(1, 2)
+        acc12 = open_tiles()
+        passes(acc12, 1, 2, 2, True, False)
+        quant_b(1, 2)
+        for r in range(4):
+            mx(acc12[r], 1, r, 1, 2, 0, KP, False, True)
+            evac("s", acc12[r], 1, r, 2, 0)
+            store(4 + r)
+
+        quant_a(0, 1)
+        acc01 = open_tiles()
+        passes(acc01, 0, 1, 1, True, False)
+        acc02 = open_tiles()
+        passes(acc02, 0, 1, 2, True, False)
+        regroup_b(0, 1)
+        quant_a(0, 2)
+        passes(acc02, 0, 2, 2, False, False)
+        regroup_b(0, 2)
+        quant_a(0, 0)
+        quant_b(0, 1)
+        for r in range(4):
+            mx(acc01[r], 0, r, 0, 1, 0, KP, False, True)
+            evac("s", acc01[r], 0, r, 1, 0)
+        mask_b_blocks(0)
+        quant_b(0, 2)
+        regroup_b(0, 0)
+        quant_b(0, 0)
+        for r in range(4):
+            mx(acc02[r], 0, r, 0, 2, 0, KP, False, True)
+            evac("s" if r % 2 else "v", acc02[r], 0, r, 2, 0)
+        for r in range(4):
+            diag_tile(0, r, "s" if r % 2 else "v")
+            store(r)

@@ -23,7 +23,7 @@ PIECES = {0: [(0, 512)], 1: [(128, 128), (256, 256)], 2: [(256, 256)], 3: [(384,
 
 
 def o_lo(i):
-    return 0 if i < 8 else 2 * KP
+    return KP * (i // 4)
 
 
 def slot(first, second):
@@ -39,13 +39,18 @@ def tile_modelnew_kernel(tc, A, B, out):
         psum = ctx.enter_context(tc.psum_pool(name="psum", bufs=1))
         ctx.enter_context(tc.manual_schedule())
 
+        ag = {}
         a_sb = {}
         o_sb = {}
         o_low = keep.tile([P, 4, KP], F32, name="o_low")
         for i in range(12):
-            a_sb[i] = keep.tile([P, N - KP * (i // 4)], BF16, name="a_sb%d" % i)
+            g, r = i // 4, i % 4
+            wid = N - KP * g
+            if r == 0:
+                ag[g] = keep.tile([P, 4 * (wid + P)], BF16, name="ag%d" % g)
+            a_sb[i] = ag[g][:, r * wid : r * wid + wid]
             if i < 8:
-                o_sb[i] = keep.tile([P, N], F32, name="o_sb%d" % i)
+                o_sb[i] = keep.tile([P, N - o_lo(i)], F32, name="o_sb%d" % i)
             else:
                 o_sb[i] = o_low[:, i - 8, :]
         b_raw = {}
@@ -62,10 +67,12 @@ def tile_modelnew_kernel(tc, A, B, out):
         b_scl = keep.tile([P, 6, KP], U8, name="b_scl", align_bytes=64)
         zeros = const.tile([P, 2 * KP], F32, name="zeros")
         ident = const.tile([P, P], F32, name="ident")
-        mf = const.tile([P, 1088], F32, name="mf")
-        mw = const.tile([P, 1088], I32, name="mw")
-        mask_a = mw[:, 0:64]
-        mask_b = mw[:, 64:1088].rearrange("p (t x) -> p t x", t=4)
+        mfa = const.tile([P, 64], F32, name="mfa")
+        mwa = const.tile([P, 64], I32, name="mwa")
+        mfb = const.tile([P, 1024], F32, name="mfb")
+        mwb = const.tile([P, 1024], I32, name="mwb")
+        mask_a = mwa[:]
+        mask_b = mwb[:].rearrange("p (t x) -> p t x", t=4)
         banks = [0]
 
         def bank(shape):
@@ -83,9 +90,10 @@ def tile_modelnew_kernel(tc, A, B, out):
             nc.sync.dma_start(out=b_raw[g][:], in_=B[k0 : k0 + KP, k0:N].rearrange("(p t) w -> p t w", t=4))
 
         def mask_a_blocks(g):
-            for r in range(4):
-                blk = a_sb[4 * g + r][:, P * r : P * r + P].bitcast(I32)
-                nc.vector.tensor_tensor(out=blk, in0=blk, in1=mask_a, op=ALU.bitwise_and)
+            blk = ag[g][:].bitcast(I32).rearrange("p (r s) -> p r s", r=4)[:, :, 0:64]
+            nc.vector.tensor_tensor(
+                out=blk, in0=blk, in1=mask_a.unsqueeze(1).to_broadcast([P, 4, 64]), op=ALU.bitwise_and
+            )
 
         def mask_b_blocks(g):
             blk = b_raw[g][:, :, 0:KP].bitcast(I32)
@@ -96,7 +104,7 @@ def tile_modelnew_kernel(tc, A, B, out):
             for b in range(2):
                 xt = bank([P, 2, 2, P])
                 for q in range(2):
-                    af = a_sb[4 * g + 2 * b + q][:].bitcast(F32)
+                    af = a_sb[4 * g + 2 * b + q].bitcast(F32)
                     for u in range(2):
                         w0 = 256 * (c - g)
                         nc.tensor.transpose(xt[:, q, u, :], af[:, w0 + u : w0 + 256 : 2], ident[:])
@@ -109,9 +117,9 @@ def tile_modelnew_kernel(tc, A, B, out):
             s = slot(g, c)
             nc.vector.quantize_mx(out=a_cod[:, s, :].bitcast(FP8X4), scales=a_scl[:, s, :], in_=ga[s][:])
 
-        def regroup_b(c, j):
+        def regroup_b(c, j, copy=nc.vector.tensor_copy):
             src = b_raw[c][:, :, KP * (j - c) : KP * (j - c) + KP]
-            nc.vector.tensor_copy(
+            copy(
                 out=gb[slot(c, j)][:].rearrange("p (c i) t -> p c t i", i=4),
                 in_=src.rearrange("p t (c i) -> p c t i", i=4),
             )
@@ -166,81 +174,92 @@ def tile_modelnew_kernel(tc, A, B, out):
         for g in (2, 1, 0):
             for r in range(1, 4):
                 nc.vector.memset(a_sb[4 * g + r][:, 0 : P * r].bitcast(I32), 0)
-        for g in (2, 1, 0):
-            load_a(g)
-            load_b(g)
+        load_b(1)
+        load_a(2)
+        load_b(2)
+        load_a(1)
+        load_a(0)
+        load_b(0)
         nc.sync.dma_start(
             out=out[2 * KP : N, 0 : 2 * KP].rearrange("(r p) w -> p r w", p=P),
             in_=zeros[:].unsqueeze(1).to_broadcast([P, 4, 2 * KP]),
         )
-        zero_prefix([9, 10, 11, 4, 5, 6, 7])
-        nc.gpsimd.memset(mf[:], -1.0)
+        nc.sync.dma_start(
+            out=out[KP : 2 * KP, 0:KP].rearrange("(r p) w -> p r w", p=P),
+            in_=zeros[:, 0:KP].unsqueeze(1).to_broadcast([P, 4, KP]),
+        )
+        zero_prefix([9, 10, 11, 5, 6, 7, 1, 2, 3])
+        nc.gpsimd.memset(mfa[:], -1.0)
         for lo_hi, fill in ((0, -65536.0), (1, 0.0)):
             nc.gpsimd.affine_select(
-                out=mf[:, 0:64], in_=mf[:, 0:64], pattern=[[2, 64]], compare_op=ALU.is_ge,
+                out=mfa[:], in_=mfa[:], pattern=[[2, 64]], compare_op=ALU.is_ge,
                 fill=fill, base=lo_hi, channel_multiplier=-1,
             )
-            nc.gpsimd.affine_select(
-                out=mf[:, 64:1088], in_=mf[:, 64:1088], pattern=[[-1, 4], [2, 256]], compare_op=ALU.is_ge,
-                fill=fill, base=lo_hi, channel_multiplier=-4,
-            )
         make_identity(nc, ident[:])
-        nc.vector.tensor_copy(out=mw[:], in_=mf[:])
+        nc.gpsimd.affine_select(
+            out=mfb[:], in_=zeros[:], pattern=[[1, 4], [-2, 256]], compare_op=ALU.is_gt,
+            fill=-65536.0, base=-1, channel_multiplier=4,
+        )
+        nc.gpsimd.affine_select(
+            out=mfb[:], in_=mfb[:], pattern=[[1, 4], [-2, 256]], compare_op=ALU.is_gt,
+            fill=-1.0, base=0, channel_multiplier=4,
+        )
+        nc.vector.tensor_copy(out=mwa[:], in_=mfa[:])
 
+        regroup_b(1, 2)
+        nc.vector.tensor_copy(out=mwb[:], in_=mfb[:])
         mask_a_blocks(2)
         transpose_a(2, 2)
-        mask_b_blocks(2)
-        regroup_b(2, 2)
+        mask_b_blocks(1)
+        quant_b(1, 2)
+        regroup_b(1, 1)
         mask_a_blocks(1)
         transpose_a(1, 1)
         transpose_a(1, 2)
-        quant_b(2, 2)
+        mask_b_blocks(2)
+        quant_b(1, 1)
+        regroup_b(2, 2)
+        mask_a_blocks(0)
+        transpose_a(0, 0)
+        transpose_a(0, 1)
         quant_a(2, 2)
+        quant_a(1, 1)
+        quant_b(2, 2)
         for r in range(4):
             diag_tile(2, r, "s")
         nc.sync.dma_start(out=out[2 * KP : N, 2 * KP : N].rearrange("(r p) w -> p r w", p=P), in_=o_low[:])
-        zero_prefix([1, 2, 3])
-
-        mask_b_blocks(1)
-        regroup_b(1, 1)
-        quant_a(1, 1)
-        regroup_b(1, 2)
-        mask_a_blocks(0)
-        for c in (1, 2, 0):
-            transpose_a(0, c)
-        quant_b(1, 1)
+        transpose_a(0, 2)
         for r in range(4):
             diag_tile(1, r, "s")
         quant_a(1, 2)
         acc12 = open_tiles()
-        passes(acc12, 1, 2, 2, True, False)
-        quant_b(1, 2)
+        passes(acc12, 1, 1, 2, True, False)
         for r in range(4):
-            mx(acc12[r], 1, r, 1, 2, 0, KP, False, True)
+            mx(acc12[r], 1, r, 2, 2, 0, KP, False, True)
             evac("s", acc12[r], 1, r, 2, 0)
             store(4 + r)
 
+        regroup_b(0, 1)
+        quant_a(0, 0)
         quant_a(0, 1)
+        quant_b(0, 1)
         acc01 = open_tiles()
         passes(acc01, 0, 1, 1, True, False)
-        acc02 = open_tiles()
-        passes(acc02, 0, 1, 2, True, False)
-        regroup_b(0, 1)
-        quant_a(0, 2)
-        passes(acc02, 0, 2, 2, False, False)
-        regroup_b(0, 2)
-        quant_a(0, 0)
-        quant_b(0, 1)
         for r in range(4):
             mx(acc01[r], 0, r, 0, 1, 0, KP, False, True)
             evac("s", acc01[r], 0, r, 1, 0)
+        regroup_b(0, 2)
+        quant_a(0, 2)
+        acc02 = open_tiles()
+        passes(acc02, 0, 1, 2, True, False)
+        passes(acc02, 0, 2, 2, False, False)
         mask_b_blocks(0)
         quant_b(0, 2)
         regroup_b(0, 0)
-        quant_b(0, 0)
         for r in range(4):
             mx(acc02[r], 0, r, 0, 2, 0, KP, False, True)
-            evac("s" if r % 2 else "v", acc02[r], 0, r, 2, 0)
+            evac("s", acc02[r], 0, r, 2, 0)
+        quant_b(0, 0)
         for r in range(4):
             diag_tile(0, r, "s" if r % 2 else "v")
             store(r)

@@ -19,13 +19,6 @@ NG = N // KP
 FLOPS = 2 * N * (N + 1) * (N + 2) // 6
 BYTES = 2 * (N * (N + 1) // 2) * 2 + N * N * 4
 
-PIECES = {0: [(0, 512)], 1: [(128, 128), (256, 256)], 2: [(256, 256)], 3: [(384, 128)]}
-
-
-def o_lo(i):
-    return KP * (i // 4)
-
-
 def slot(first, second):
     base = {2: 0, 1: 1, 0: 3}
     return base[first] + second - first
@@ -42,17 +35,14 @@ def tile_modelnew_kernel(tc, A, B, out):
         ag = {}
         a_sb = {}
         o_sb = {}
-        o_low = keep.tile([P, 4, KP], F32, name="o_low")
         for i in range(12):
             g, r = i // 4, i % 4
             wid = N - KP * g
             if r == 0:
                 ag[g] = keep.tile([P, 4 * (wid + P)], BF16, name="ag%d" % g)
             a_sb[i] = ag[g][:, r * wid : r * wid + wid]
-            if i < 8:
-                o_sb[i] = keep.tile([P, N - o_lo(i)], F32, name="o_sb%d" % i)
-            else:
-                o_sb[i] = o_low[:, i - 8, :]
+        for h in range(6):
+            o_sb[h] = keep.tile([P, 2, N if h < 4 else KP], F32, name="o_sb%d" % h)
         b_raw = {}
         for c in range(NG):
             b_raw[c] = keep.tile([P, 4, N - KP * c], BF16, name="b_raw%d" % c)
@@ -67,12 +57,11 @@ def tile_modelnew_kernel(tc, A, B, out):
         b_scl = keep.tile([P, 6, KP], U8, name="b_scl", align_bytes=64)
         zeros = const.tile([P, 2 * KP], F32, name="zeros")
         ident = const.tile([P, P], F32, name="ident")
-        mfa = const.tile([P, 64], F32, name="mfa")
-        mwa = const.tile([P, 64], I32, name="mwa")
-        mfb = const.tile([P, 1024], F32, name="mfb")
-        mwb = const.tile([P, 1024], I32, name="mwb")
-        mask_a = mwa[:]
-        mask_b = mwb[:].rearrange("p (t x) -> p t x", t=4)
+        dist = const.tile([P, 64 + 2 * 257], I32, name="dist")
+        mf = const.tile([P, 64 + 2 * 257], F32, name="mf")
+        mw = const.tile([P, 64 + 2 * 257], I32, name="mw")
+        mask_a = mw[:, 0:64]
+        mask_b = mw[:, 64:].rearrange("p (t x) -> p t x", t=2)
         banks = [0]
 
         def bank(shape):
@@ -96,21 +85,22 @@ def tile_modelnew_kernel(tc, A, B, out):
             )
 
         def mask_b_blocks(g):
-            blk = b_raw[g][:, :, 0:KP].bitcast(I32)
-            nc.vector.tensor_tensor(out=blk, in0=blk, in1=mask_b, op=ALU.bitwise_and)
+            for u in range(2):
+                blk = b_raw[g][:, 2 * u : 2 * u + 2, 0:KP].bitcast(I32)
+                nc.vector.tensor_tensor(out=blk, in0=blk, in1=mask_b[:, :, 1 - u : 257 - u], op=ALU.bitwise_and)
 
         def transpose_a(g, c):
             gaf = ga[slot(g, c)][:].bitcast(F32)
             for b in range(2):
-                xt = bank([P, 2, 2, P])
+                xt = bank([P, 2, 2 * P])
                 for q in range(2):
                     af = a_sb[4 * g + 2 * b + q].bitcast(F32)
                     for u in range(2):
                         w0 = 256 * (c - g)
-                        nc.tensor.transpose(xt[:, q, u, :], af[:, w0 + u : w0 + 256 : 2], ident[:])
+                        nc.tensor.transpose(xt[:, u, P * q : P * q + P], af[:, w0 + u : w0 + 256 : 2], ident[:])
                 nc.scalar.copy(
-                    out=gaf[:, 512 * b : 512 * b + 512].rearrange("p (q i u) -> p q i u", q=2, u=2),
-                    in_=xt[:].rearrange("p q u i -> p q i u"),
+                    out=gaf[:, 512 * b : 512 * b + 512].rearrange("p (r x u) -> p r x u", r=2, u=2),
+                    in_=xt[:].rearrange("p u (x r) -> p r x u", r=2),
                 )
 
         def quant_a(g, c):
@@ -143,8 +133,8 @@ def tile_modelnew_kernel(tc, A, B, out):
             )
 
         def evac(eng, acc, g, r, j, lo):
-            i = 4 * g + r
-            dst = o_sb[i][:, KP * j + lo - o_lo(i) : KP * j + KP - o_lo(i)]
+            c0 = KP * j if g < 2 else 0
+            dst = o_sb[2 * g + r // 2][:, r % 2, c0 + lo : c0 + KP]
             if eng == "v":
                 nc.vector.tensor_copy(out=dst, in_=acc[:, lo:KP])
             else:
@@ -152,9 +142,9 @@ def tile_modelnew_kernel(tc, A, B, out):
 
         def diag_tile(g, r, eng):
             acc = bank([P, KP])
-            for off, wid in PIECES[r]:
-                mx(acc, g, r, g, g, off, wid, True, True)
-            evac(eng, acc, g, r, g, P * r)
+            lo = 256 * (r // 2)
+            mx(acc, g, r, g, g, lo, KP - lo, True, True)
+            evac(eng, acc, g, r, g, lo)
 
         def open_tiles():
             return [bank([P, KP]) for r in range(4)]
@@ -163,103 +153,97 @@ def tile_modelnew_kernel(tc, A, B, out):
             for r in range(4):
                 mx(accs[r], g, r, c, j, 0, KP, start, stop)
 
-        def zero_prefix(rows):
-            for i in rows:
-                nc.scalar.copy(out=o_sb[i][:, 0 : P * i - o_lo(i)], in_=zeros[:, 0 : P * i - o_lo(i)])
+        def zero(dst):
+            nc.scalar.copy(out=dst, in_=zeros[:, 0 : dst.shape[2]].unsqueeze(1).to_broadcast(list(dst.shape)))
 
-        def store(i):
-            nc.sync.dma_start(out=out[P * i : P * i + P, o_lo(i) : N], in_=o_sb[i][:])
+        def store(h):
+            lo = 0 if h < 4 else 2 * KP
+            nc.sync.dma_start(
+                out=out[256 * h : 256 * h + 256, lo:N].rearrange("(p r) w -> p r w", r=2), in_=o_sb[h][:]
+            )
 
+        nc.gpsimd.iota(dist[:, 0:64], pattern=[[2, 64]], base=0, channel_multiplier=-1)
+        nc.gpsimd.iota(dist[:, 64:], pattern=[[-1, 2], [2, 257]], base=-2, channel_multiplier=-4)
         nc.vector.memset(zeros[:], 0.0)
-        for g in (2, 1, 0):
+        for r in range(1, 4):
+            nc.gpsimd.memset(a_sb[8 + r][:, 0 : P * r].bitcast(I32), 0)
+        make_identity(nc, ident[:])
+        for g in (1, 0):
             for r in range(1, 4):
-                nc.vector.memset(a_sb[4 * g + r][:, 0 : P * r].bitcast(I32), 0)
-        load_b(1)
-        load_a(2)
+                nc.gpsimd.memset(a_sb[4 * g + r][:, 0 : P * r].bitcast(I32), 0)
         load_b(2)
+        load_a(2)
+        load_b(1)
         load_a(1)
-        load_a(0)
         load_b(0)
+        load_a(0)
         nc.sync.dma_start(
             out=out[2 * KP : N, 0 : 2 * KP].rearrange("(r p) w -> p r w", p=P),
             in_=zeros[:].unsqueeze(1).to_broadcast([P, 4, 2 * KP]),
         )
-        nc.sync.dma_start(
-            out=out[KP : 2 * KP, 0:KP].rearrange("(r p) w -> p r w", p=P),
-            in_=zeros[:, 0:KP].unsqueeze(1).to_broadcast([P, 4, KP]),
-        )
-        zero_prefix([9, 10, 11, 5, 6, 7, 1, 2, 3])
-        nc.gpsimd.memset(mfa[:], -1.0)
-        for lo_hi, fill in ((0, -65536.0), (1, 0.0)):
-            nc.gpsimd.affine_select(
-                out=mfa[:], in_=mfa[:], pattern=[[2, 64]], compare_op=ALU.is_ge,
-                fill=fill, base=lo_hi, channel_multiplier=-1,
-            )
-        make_identity(nc, ident[:])
-        nc.gpsimd.affine_select(
-            out=mfb[:], in_=zeros[:], pattern=[[1, 4], [-2, 256]], compare_op=ALU.is_gt,
-            fill=-65536.0, base=-1, channel_multiplier=4,
-        )
-        nc.gpsimd.affine_select(
-            out=mfb[:], in_=mfb[:], pattern=[[1, 4], [-2, 256]], compare_op=ALU.is_gt,
-            fill=-1.0, base=0, channel_multiplier=4,
-        )
-        nc.vector.tensor_copy(out=mwa[:], in_=mfa[:])
+        zero(o_sb[5][:, :, 0:256])
+        zero(o_sb[2][:, :, 0:512])
+        zero(o_sb[3][:, :, 0:768])
+        zero(o_sb[1][:, :, 0:256])
+        nc.vector.tensor_scalar(out=mf[:], in0=dist[:], scalar1=-1.0 / 65536, scalar2=65536.0, op0=ALU.min, op1=ALU.mult)
+        nc.vector.scalar_tensor_tensor(out=mw[:], in0=dist[:], scalar=-1.0, in1=mf[:], op0=ALU.is_ge, op1=ALU.mult)
 
-        regroup_b(1, 2)
-        nc.vector.tensor_copy(out=mwb[:], in_=mfb[:])
+        mask_b_blocks(2)
         mask_a_blocks(2)
         transpose_a(2, 2)
+        regroup_b(2, 2)
         mask_b_blocks(1)
-        quant_b(1, 2)
-        regroup_b(1, 1)
+        quant_b(2, 2)
+        quant_a(2, 2)
+        regroup_b(1, 2, nc.scalar.copy)
+
         mask_a_blocks(1)
         transpose_a(1, 1)
         transpose_a(1, 2)
-        mask_b_blocks(2)
-        quant_b(1, 1)
-        regroup_b(2, 2)
-        mask_a_blocks(0)
-        transpose_a(0, 0)
-        transpose_a(0, 1)
-        quant_a(2, 2)
-        quant_a(1, 1)
-        quant_b(2, 2)
+        regroup_b(1, 1)
         for r in range(4):
             diag_tile(2, r, "s")
-        nc.sync.dma_start(out=out[2 * KP : N, 2 * KP : N].rearrange("(r p) w -> p r w", p=P), in_=o_low[:])
-        transpose_a(0, 2)
+        store(4)
+        store(5)
+        quant_b(1, 2)
+        quant_b(1, 1)
+        mask_b_blocks(0)
+        quant_a(1, 1)
+        quant_a(1, 2)
         for r in range(4):
             diag_tile(1, r, "s")
-        quant_a(1, 2)
         acc12 = open_tiles()
         passes(acc12, 1, 1, 2, True, False)
         for r in range(4):
             mx(acc12[r], 1, r, 2, 2, 0, KP, False, True)
             evac("s", acc12[r], 1, r, 2, 0)
-            store(4 + r)
+        store(2)
+        store(3)
+        mask_a_blocks(0)
+        for c in range(NG):
+            transpose_a(0, c)
 
-        regroup_b(0, 1)
-        quant_a(0, 0)
-        quant_a(0, 1)
-        quant_b(0, 1)
-        acc01 = open_tiles()
-        passes(acc01, 0, 1, 1, True, False)
-        for r in range(4):
-            mx(acc01[r], 0, r, 0, 1, 0, KP, False, True)
-            evac("s", acc01[r], 0, r, 1, 0)
-        regroup_b(0, 2)
-        quant_a(0, 2)
-        acc02 = open_tiles()
-        passes(acc02, 0, 1, 2, True, False)
-        passes(acc02, 0, 2, 2, False, False)
-        mask_b_blocks(0)
-        quant_b(0, 2)
         regroup_b(0, 0)
-        for r in range(4):
-            mx(acc02[r], 0, r, 0, 2, 0, KP, False, True)
-            evac("s", acc02[r], 0, r, 2, 0)
+        regroup_b(0, 1)
+        regroup_b(0, 2)
         quant_b(0, 0)
+        quant_b(0, 1)
+        quant_a(0, 0)
         for r in range(4):
-            diag_tile(0, r, "s" if r % 2 else "v")
-            store(r)
+            diag_tile(0, r, "s")
+        quant_b(0, 2)
+        quant_a(0, 1)
+        quant_a(0, 2)
+        for b in range(2):
+            for r in (2 * b, 2 * b + 1):
+                acc = bank([P, KP])
+                mx(acc, 0, r, 0, 1, 0, KP, True, False)
+                mx(acc, 0, r, 1, 1, 0, KP, False, True)
+                evac("v", acc, 0, r, 1, 0)
+            for r in (2 * b, 2 * b + 1):
+                acc = bank([P, KP])
+                mx(acc, 0, r, 0, 2, 0, KP, True, False)
+                mx(acc, 0, r, 1, 2, 0, KP, False, False)
+                mx(acc, 0, r, 2, 2, 0, KP, False, True)
+                evac("s", acc, 0, r, 2, 0)
+            store(b)

from contextlib import ExitStack

import concourse.mybir as mybir
from concourse.masks import make_identity

FP8X4 = mybir.dt.float8_e4m3fn_x4
BF16 = mybir.dt.bfloat16
F32 = mybir.dt.float32
I32 = mybir.dt.int32
U32 = mybir.dt.uint32
U8 = mybir.dt.uint8
ALU = mybir.AluOpType

N = 1536
P = 128
KP = 512
NG = N // KP

FLOPS = 2 * N * (N + 1) * (N + 2) // 6
BYTES = 2 * (N * (N + 1) // 2) * 2 + N * N * 4

def slot(first, second):
    base = {2: 0, 1: 1, 0: 3}
    return base[first] + second - first


def tile_modelnew_kernel(tc, A, B, out):
    nc = tc.nc
    with ExitStack() as ctx:
        const = ctx.enter_context(tc.tile_pool(name="const", bufs=1))
        keep = ctx.enter_context(tc.tile_pool(name="keep", bufs=1))
        psum = ctx.enter_context(tc.psum_pool(name="psum", bufs=1))
        ctx.enter_context(tc.manual_schedule())

        ag = {}
        a_sb = {}
        o_sb = {}
        for i in range(12):
            g, r = i // 4, i % 4
            wid = N - KP * g
            if r == 0:
                ag[g] = keep.tile([P, 4 * (wid + P)], BF16, name="ag%d" % g)
            a_sb[i] = ag[g][:, r * wid : r * wid + wid]
        for h in range(6):
            o_sb[h] = keep.tile([P, 2, N if h < 4 else KP], F32, name="o_sb%d" % h)
        b_raw = {}
        for c in range(NG):
            b_raw[c] = keep.tile([P, 4, N - KP * c], BF16, name="b_raw%d" % c)
        ga = {}
        gb = {}
        for s in range(6):
            ga[s] = keep.tile([P, 4 * KP], BF16, name="ga%d" % s, align_bytes=64)
            gb[s] = keep.tile([P, KP, 4], BF16, name="gb%d" % s, align_bytes=64)
        a_cod = keep.tile([P, 6, KP], U32, name="a_cod", align_bytes=64)
        a_scl = keep.tile([P, 6, KP], U8, name="a_scl", align_bytes=64)
        b_cod = keep.tile([P, 6, KP], U32, name="b_cod", align_bytes=64)
        b_scl = keep.tile([P, 6, KP], U8, name="b_scl", align_bytes=64)
        zeros = const.tile([P, 2 * KP], F32, name="zeros")
        ident = const.tile([P, P], F32, name="ident")
        dist = const.tile([P, 64 + 2 * 257], I32, name="dist")
        mf = const.tile([P, 64 + 2 * 257], F32, name="mf")
        mw = const.tile([P, 64 + 2 * 257], I32, name="mw")
        mask_a = mw[:, 0:64]
        mask_b = mw[:, 64:].rearrange("p (t x) -> p t x", t=2)
        banks = [0]

        def bank(shape):
            n = banks[0]
            banks[0] = n + 1
            return psum.tile(shape, F32, name="bk%d_%d" % (n % 8, n), tag="bk%d" % (n % 8))

        def load_a(g):
            for r in range(4):
                i = 4 * g + r
                nc.sync.dma_start(out=a_sb[i][:, P * r :], in_=A[P * i : P * i + P, P * i : N])

        def load_b(g):
            k0 = KP * g
            nc.sync.dma_start(out=b_raw[g][:], in_=B[k0 : k0 + KP, k0:N].rearrange("(p t) w -> p t w", t=4))

        def mask_a_blocks(g):
            blk = ag[g][:].bitcast(I32).rearrange("p (r s) -> p r s", r=4)[:, :, 0:64]
            nc.vector.tensor_tensor(
                out=blk, in0=blk, in1=mask_a.unsqueeze(1).to_broadcast([P, 4, 64]), op=ALU.bitwise_and
            )

        def mask_b_blocks(g):
            for u in range(2):
                blk = b_raw[g][:, 2 * u : 2 * u + 2, 0:KP].bitcast(I32)
                nc.vector.tensor_tensor(out=blk, in0=blk, in1=mask_b[:, :, 1 - u : 257 - u], op=ALU.bitwise_and)

        def transpose_a(g, c):
            gaf = ga[slot(g, c)][:].bitcast(F32)
            for b in range(2):
                xt = bank([P, 2, 2 * P])
                for q in range(2):
                    af = a_sb[4 * g + 2 * b + q].bitcast(F32)
                    for u in range(2):
                        w0 = 256 * (c - g)
                        nc.tensor.transpose(xt[:, u, P * q : P * q + P], af[:, w0 + u : w0 + 256 : 2], ident[:])
                nc.scalar.copy(
                    out=gaf[:, 512 * b : 512 * b + 512].rearrange("p (r x u) -> p r x u", r=2, u=2),
                    in_=xt[:].rearrange("p u (x r) -> p r x u", r=2),
                )

        def quant_a(g, c):
            s = slot(g, c)
            nc.vector.quantize_mx(out=a_cod[:, s, :].bitcast(FP8X4), scales=a_scl[:, s, :], in_=ga[s][:])

        def regroup_b(c, j, copy=nc.vector.tensor_copy):
            src = b_raw[c][:, :, KP * (j - c) : KP * (j - c) + KP]
            copy(
                out=gb[slot(c, j)][:].rearrange("p (c i) t -> p c t i", i=4),
                in_=src.rearrange("p t (c i) -> p c t i", i=4),
            )

        def quant_b(c, j):
            s = slot(c, j)
            nc.vector.quantize_mx(
                out=b_cod[:, s, :].bitcast(FP8X4), scales=b_scl[:, s, :],
                in_=gb[s][:].rearrange("p w t -> p (w t)"),
            )

        def mx(acc, g, r, c, j, off, wid, start, stop):
            sa = slot(g, c)
            sb = slot(c, j)
            rows = slice(P * r, P * r + P)
            nc.tensor.matmul_mx(
                out=acc[:, off : off + wid],
                lhsT=a_cod[:, sa, rows].bitcast(FP8X4), lhsT_scale=a_scl[:, sa, rows],
                rhs=b_cod[:, sb, off : off + wid].bitcast(FP8X4), rhs_scale=b_scl[:, sb, off : off + wid],
                start=start, stop=stop,
            )

        def evac(eng, acc, g, r, j, lo):
            c0 = KP * j if g < 2 else 0
            dst = o_sb[2 * g + r // 2][:, r % 2, c0 + lo : c0 + KP]
            if eng == "v":
                nc.vector.tensor_copy(out=dst, in_=acc[:, lo:KP])
            else:
                nc.scalar.copy(out=dst, in_=acc[:, lo:KP])

        def diag_tile(g, r, eng):
            acc = bank([P, KP])
            lo = 256 * (r // 2)
            mx(acc, g, r, g, g, lo, KP - lo, True, True)
            evac(eng, acc, g, r, g, lo)

        def open_tiles():
            return [bank([P, KP]) for r in range(4)]

        def passes(accs, g, c, j, start, stop):
            for r in range(4):
                mx(accs[r], g, r, c, j, 0, KP, start, stop)

        def zero(dst):
            nc.scalar.copy(out=dst, in_=zeros[:, 0 : dst.shape[2]].unsqueeze(1).to_broadcast(list(dst.shape)))

        def store(h):
            lo = 0 if h < 4 else 2 * KP
            nc.sync.dma_start(
                out=out[256 * h : 256 * h + 256, lo:N].rearrange("(p r) w -> p r w", r=2), in_=o_sb[h][:]
            )

        nc.gpsimd.iota(dist[:, 0:64], pattern=[[2, 64]], base=0, channel_multiplier=-1)
        nc.gpsimd.iota(dist[:, 64:], pattern=[[-1, 2], [2, 257]], base=-2, channel_multiplier=-4)
        nc.vector.memset(zeros[:], 0.0)
        for r in range(1, 4):
            nc.gpsimd.memset(a_sb[8 + r][:, 0 : P * r].bitcast(I32), 0)
        make_identity(nc, ident[:])
        for g in (1, 0):
            for r in range(1, 4):
                nc.gpsimd.memset(a_sb[4 * g + r][:, 0 : P * r].bitcast(I32), 0)
        load_b(2)
        load_a(2)
        load_b(1)
        load_a(1)
        load_b(0)
        load_a(0)
        nc.sync.dma_start(
            out=out[2 * KP : N, 0 : 2 * KP].rearrange("(r p) w -> p r w", p=P),
            in_=zeros[:].unsqueeze(1).to_broadcast([P, 4, 2 * KP]),
        )
        zero(o_sb[5][:, :, 0:256])
        zero(o_sb[2][:, :, 0:512])
        zero(o_sb[3][:, :, 0:768])
        zero(o_sb[1][:, :, 0:256])
        nc.vector.tensor_scalar(out=mf[:], in0=dist[:], scalar1=-1.0 / 65536, scalar2=65536.0, op0=ALU.min, op1=ALU.mult)
        nc.vector.scalar_tensor_tensor(out=mw[:], in0=dist[:], scalar=-1.0, in1=mf[:], op0=ALU.is_ge, op1=ALU.mult)

        mask_b_blocks(2)
        mask_a_blocks(2)
        transpose_a(2, 2)
        regroup_b(2, 2)
        mask_b_blocks(1)
        quant_b(2, 2)
        quant_a(2, 2)
        regroup_b(1, 2, nc.scalar.copy)

        mask_a_blocks(1)
        transpose_a(1, 1)
        transpose_a(1, 2)
        regroup_b(1, 1)
        for r in range(4):
            diag_tile(2, r, "s")
        store(4)
        store(5)
        quant_b(1, 2)
        quant_b(1, 1)
        mask_b_blocks(0)
        quant_a(1, 1)
        quant_a(1, 2)
        for r in range(4):
            diag_tile(1, r, "s")
        acc12 = open_tiles()
        passes(acc12, 1, 1, 2, True, False)
        for r in range(4):
            mx(acc12[r], 1, r, 2, 2, 0, KP, False, True)
            evac("s", acc12[r], 1, r, 2, 0)
        store(2)
        store(3)
        mask_a_blocks(0)
        for c in range(NG):
            transpose_a(0, c)

        regroup_b(0, 0)
        regroup_b(0, 1)
        regroup_b(0, 2)
        quant_b(0, 0)
        quant_b(0, 1)
        quant_a(0, 0)
        for r in range(4):
            diag_tile(0, r, "s")
        quant_b(0, 2)
        quant_a(0, 1)
        quant_a(0, 2)
        for b in range(2):
            for r in (2 * b, 2 * b + 1):
                acc = bank([P, KP])
                mx(acc, 0, r, 0, 1, 0, KP, True, False)
                mx(acc, 0, r, 1, 1, 0, KP, False, True)
                evac("v", acc, 0, r, 1, 0)
            for r in (2 * b, 2 * b + 1):
                acc = bank([P, KP])
                mx(acc, 0, r, 0, 2, 0, KP, True, False)
                mx(acc, 0, r, 1, 2, 0, KP, False, False)
                mx(acc, 0, r, 2, 2, 0, KP, False, True)
                evac("s", acc, 0, r, 2, 0)
            store(b)
